import numpy as np
import ml_dtypes


def mxq(x, axis, fmt="e4m3"):
    dtype, down = {"e4m3": (ml_dtypes.float8_e4m3fn, 7), "e5m2": (ml_dtypes.float8_e5m2, 14)}[fmt]
    v = np.moveaxis(np.asarray(x, np.float32).astype(ml_dtypes.bfloat16).astype(np.float64), axis, -1)
    blocks = v.reshape(v.shape[:-1] + (-1, 32))
    amax = np.abs(blocks).max(-1, keepdims=True)
    byte = np.maximum(np.where(amax > 0, np.frexp(amax)[1] - 1 + 127, 0) - down, 1)
    scale = np.exp2(byte - 127.0)
    codes = (blocks / scale).astype(np.float32).astype(dtype).astype(np.float64)
    return np.moveaxis((codes * scale).reshape(v.shape), -1, axis)


WIDE = False


def mx_kscale(k):
    if not WIDE:
        return np.ones(k)
    levels = np.array([10, -10, 5, -5, 0])
    if k % 512:
        return np.exp2(np.random.permutation(np.resize(levels, k // 32))).repeat(32)
    a = np.empty((k // 512, 16))
    for p in range(k // 512):
        a[p, :8] = np.random.permutation(np.resize(levels, 8))
        for g in range(8):
            far = levels[np.abs(levels - a[p, g]) >= 10]
            a[p, g + 8] = far[np.random.randint(len(far))]
    return np.exp2(a.ravel()).repeat(32)


BF16 = ml_dtypes.bfloat16


def bf(x):
    return np.asarray(x, np.float32).astype(BF16)


def f64(x):
    return np.asarray(x).astype(np.float64)


B, N, D, H, L, C = 4, 512, 512, 8, 3, 2
HD = D // H


def setup_inputs():
    s, t = mx_kscale(D), mx_kscale(D)
    tk = t.reshape(H, HD)[:, :L]
    return {
        "fields": bf((np.random.standard_normal((B, N, D)) + np.random.standard_normal((B, 1, D))) * t),
        "h2": bf(np.maximum(np.random.standard_normal((B, N, D)), 0.0) * 1.4 * s),
        "corr_kernels": bf(np.random.standard_normal((H, L, L)) * 2.5 / tk[:, None, :]),
        "w3": bf(np.random.standard_normal((D, D)) * 1.5 / np.sqrt(D) * t[:, None] / s[None, :]),
        "b3": bf(np.random.standard_normal(D) * 0.3 * t),
        "out_w": bf(np.random.standard_normal((D, D)) / np.sqrt(D) / t[None, :]),
        "out_b": bf(np.random.standard_normal(D) * 0.3),
        "inter_w": bf(1.0 + 0.5 * np.random.standard_normal(C)),
    }


def reference(fields, h2, corr_kernels, w3, b3, out_w, out_b, inter_w):
    f = f64(fields).reshape(B, N, H, HD)
    ck = f64(corr_kernels)
    corr = np.zeros((B, N, H, HD))
    for lag in range(1, L + 1):
        base = f[:, :-lag]
        shifted = f[:, lag:]
        w = np.pad(ck[:, lag - 1, :], ((0, 0), (0, HD - L)))
        mean_shift = shifted.mean(axis=1, keepdims=True)
        cw = base * w[None, None] * mean_shift
        corr = corr + np.pad(cw, ((0, 0), (0, lag), (0, 0), (0, 0)))
    corr = corr / L
    nl = (f64(bf(mxq(f64(h2), 2, "e4m3") @ mxq(f64(w3), 1, "e4m3").T)) + f64(b3)).reshape(B, N, H, HD)
    r = f64(inter_w)
    e = np.exp(r - r.max())
    iw = e / e.sum()
    enhanced = (f + iw[0] * corr + iw[1] * nl).reshape(B, N, D)
    return (mxq(enhanced, 2, "e4m3") @ mxq(f64(out_w), 1, "e4m3").T) + f64(out_b)

@@ -1,0 +1,353 @@
+from contextlib import ExitStack
+
+import concourse.masks as masks
+import concourse.mybir as mybir
+
+F32 = mybir.dt.float32
+BF16 = mybir.dt.bfloat16
+U32 = mybir.dt.uint32
+U8 = mybir.dt.uint8
+FP8X4 = mybir.dt.float8_e4m3fn_x4
+ALU = mybir.AluOpType
+ACT = mybir.ActivationFunctionType
+AX = mybir.AxisListType
+
+B, N, D, H, L = 4, 512, 512, 8, 3
+P = 128
+S4 = 4
+NT = B * S4
+NK = NT // 2
+FLOPS = 2 * 2 * B * N * D * D
+BANK_DT = BF16
+OFF = (1, 3, 5, 7, 9, 11, 13)
+
+
+def tile_fieldinteractionoperators_pa_kernel(
+    tc, fields, h2, corr_kernels, w3, b3, out_w, out_b, inter_w, out
+):
+    nc = tc.nc
+    V = nc.vector
+    G = nc.gpsimd
+    with ExitStack() as ctx:
+        const = ctx.enter_context(tc.tile_pool(name="const", bufs=1))
+        loads = ctx.enter_context(tc.tile_pool(name="loads", bufs=1))
+        work = ctx.enter_context(tc.tile_pool(name="work", bufs=2))
+        small = ctx.enter_context(tc.tile_pool(name="small", bufs=2))
+        psum = ctx.enter_context(tc.psum_pool(name="psum", bufs=2))
+        ctx.enter_context(tc.manual_schedule())
+
+        w3_sb = loads.tile([P, S4, D], BF16, name="w3_sb")
+        ow_sb = loads.tile([P, S4, D], BF16, name="ow_sb")
+        h2_sb = [loads.tile([P, S4, D], BF16, name="h2_sb%d" % b) for b in range(B)]
+        f_sb = [loads.tile([P, S4, D], BF16, name="f_sb%d" % b) for b in range(B)]
+        w3_v = w3.rearrange("(m t) k -> m t k", t=S4)
+        ow_v = out_w.rearrange("(r m) c -> m r c", m=P)
+        h2_v = [h2[b].rearrange("(p j) k -> p j k", j=S4) for b in range(B)]
+        f_v = [fields[b].rearrange("(p j) c -> p j c", j=S4) for b in range(B)]
+        r_bf = const.tile([P, 2], BF16, name="r_bf")
+        b3_bf = const.tile([P, S4], BF16, name="b3_bf")
+        kk_bf = const.tile([P, L, S4], BF16, name="kk_bf")
+        ht_bf = const.tile([P, 2 * L, B, S4], BF16, name="ht_bf")
+        zrow = const.tile([P, D], BF16, name="zrow")
+        ones_bf = const.tile([P, P], BF16, name="ones_bf")
+        ident = const.tile([P, P], F32, name="ident")
+        dm0 = const.tile([P, 1], F32, name="dm0")
+        dm1 = const.tile([P, 1], F32, name="dm1")
+
+        V.memset(dm0[:], 0.0)
+        nc.scalar.activation(out=dm1[:], in_=dm0[:], func=ACT.Exp)
+        V.memset(kk_bf[:], 0.0)
+        V.memset(ht_bf[:], 0.0)
+        V.memset(ones_bf[:], 1.0)
+        V.memset(zrow[:], 0.0)
+
+        def load_half(dst, src, half):
+            sl = slice(2 * half, 2 * half + 2)
+            nc.sync.dma_start(out=dst[:, sl, :], in_=src[:, sl, :])
+
+        def load_row(q, x):
+            n = x if x < L else N - 2 * L + x
+            rv = fields[:, n, :].rearrange("b (h r) -> h b r", r=D // H)
+            q.dma_start(out=ht_bf[0:P:16, x, :, :], in_=rv[:, :, 0:S4])
+
+        G.dma_start(out=b3_bf[:], in_=b3.rearrange("(p t) -> p t", t=S4))
+        masks.make_identity(nc, ident[:])
+        nc.sync.dma_start(out=r_bf[:], in_=inter_w.partition_broadcast(P))
+        nc.sync.dma_start(out=kk_bf[0:P:16, :, 0:L], in_=corr_kernels)
+        for x in range(L):
+            load_row(nc.sync, x)
+        load_half(w3_sb, w3_v, 0)
+        load_half(w3_sb, w3_v, 1)
+        load_half(h2_sb[0], h2_v[0], 0)
+        nc.sync.dma_start(out=f_sb[0][:], in_=f_v[0])
+        load_half(h2_sb[0], h2_v[0], 1)
+        nc.sync.dma_start(out=ow_sb[:], in_=ow_v)
+        nc.sync.dma_start(out=f_sb[1][:], in_=f_v[1])
+        load_half(h2_sb[1], h2_v[1], 0)
+        load_half(h2_sb[1], h2_v[1], 1)
+        for b in range(2, B):
+            nc.sync.dma_start(out=f_sb[b][:], in_=f_v[b])
+            nc.sync.dma_start(out=h2_sb[b][:], in_=h2_v[b])
+        for x in range(L, 2 * L):
+            load_row(G, x)
+        G.dma_start(out=zrow[0:1, :], in_=out_b.rearrange("(a o) -> a o", a=1))
+
+        rmax = const.tile([P, 1], F32, name="rmax")
+        rd = const.tile([P, 2], F32, name="rd")
+        re = const.tile([P, 2], F32, name="re")
+        rsum = const.tile([P, 1], F32, name="rsum")
+        rinv = const.tile([P, 1], F32, name="rinv")
+        iw = const.tile([P, 2], F32, name="iw")
+        bb = const.tile([P, S4], F32, name="bb")
+        kap = const.tile([P, L, S4], F32, name="kap")
+        tt = const.tile([P, S4, S4], F32, name="tt")
+        hh = const.tile([P, L, B, S4], F32, name="hh")
+        qq = const.tile([P, L, B, S4], F32, name="qq")
+        uu = const.tile([P, S4, B, S4], F32, name="uu")
+        bias_sb = const.tile([P, D], F32, name="bias_sb")
+        V.tensor_reduce(out=rmax[:], in_=r_bf[:], axis=AX.X, op=ALU.max)
+        V.tensor_scalar(out=rd[:], in0=r_bf[:], scalar1=rmax[:, 0:1], scalar2=None, op0=ALU.subtract)
+        nc.scalar.activation(out=re[:], in_=rd[:], func=ACT.Exp, accum_out=rsum[:])
+        V.reciprocal(out=rinv[:], in_=rsum[:])
+        V.tensor_scalar(out=iw[:], in0=re[:], scalar1=rinv[:, 0:1], scalar2=None, op0=ALU.mult)
+        for lag in range(1, L + 1):
+            V.tensor_scalar(
+                out=kap[:, lag - 1, :], in0=kk_bf[:, lag - 1, :], scalar1=iw[:, 0:1],
+                scalar2=1.0 / (L * (N - lag)), op0=ALU.mult, op1=ALU.mult,
+            )
+        V.tensor_copy(out=tt[:, 1, :], in_=kap[:, 2, :])
+        V.tensor_tensor(out=tt[:, 2, :], in0=kap[:, 1, :], in1=tt[:, 1, :], op=ALU.add)
+        V.tensor_tensor(out=tt[:, 3, :], in0=kap[:, 0, :], in1=tt[:, 2, :], op=ALU.add)
+        V.tensor_copy(out=tt[:, 0, :], in_=tt[:, 3, :])
+        V.tensor_copy(out=hh[:, 0, :, :], in_=ht_bf[:, 0, :, :])
+        V.tensor_tensor(out=hh[:, 1, :, :], in0=hh[:, 0, :, :], in1=ht_bf[:, 1, :, :], op=ALU.add)
+        V.tensor_tensor(out=hh[:, 2, :, :], in0=hh[:, 1, :, :], in1=ht_bf[:, 2, :, :], op=ALU.add)
+        V.tensor_tensor(
+            out=qq[:], in0=hh[:], in1=kap[:].unsqueeze(2).to_broadcast([P, L, B, S4]), op=ALU.mult
+        )
+        V.tensor_copy(out=uu[:, 1, :, :], in_=qq[:, 2, :, :])
+        V.tensor_tensor(out=uu[:, 2, :, :], in0=qq[:, 1, :, :], in1=uu[:, 1, :, :], op=ALU.add)
+        V.tensor_tensor(out=uu[:, 3, :, :], in0=qq[:, 0, :, :], in1=uu[:, 2, :, :], op=ALU.add)
+        V.tensor_scalar(out=uu[:, 0, :, :], in0=uu[:, 3, :, :], scalar1=-1.0, scalar2=None, op0=ALU.add)
+
+        def mx_tiles(nm):
+            c = const.tile([P, D], U32, name=nm + "_c", align_bytes=64)
+            s = const.tile([P, D], U8, name=nm + "_s", align_bytes=64)
+            return c, s
+
+        w3q = mx_tiles("w3")
+        owq = mx_tiles("ow")
+        h2q = [mx_tiles("h2_%d" % b) for b in range(B)]
+        enq = [mx_tiles("en_%d" % b) for b in range(B)]
+        grp = {}
+        gts = {}
+        sbs = {}
+        wts = {}
+        gfs = {}
+        nls = {}
+        pos = {}
+        osb = {}
+
+        def new_grp(key, tag):
+            grp[key] = work.tile([P, 4 * D], BF16, tag=tag, name=tag, align_bytes=64)
+
+        def turn(src, key, half, eng):
+            words = src[:].bitcast(F32)
+            gw = grp[key][:].bitcast(F32)
+            tp = psum.tile([P, 2, 2, P], F32, tag="tr", name="tp", bufs=3)
+            for s2 in range(2):
+                for u in range(2):
+                    nc.tensor.transpose(tp[:, s2, u, :], words[:, 2 * half + s2, u:D // 2:2], ident[:])
+            dst = gw[:, 512 * half:512 * (half + 1)].rearrange("p (s m u) -> p s m u", s=2, u=2)
+            if eng == "S":
+                nc.scalar.copy(out=dst, in_=tp[:].rearrange("p s u m -> p s m u"))
+            else:
+                V.tensor_copy(out=dst, in_=tp[:].rearrange("p s u m -> p s m u"))
+
+        def quant(key, q, lo, hi):
+            V.quantize_mx(
+                out=q[0][:, lo:hi].bitcast(FP8X4), scales=q[1][:, lo:hi], in_=grp[key][:, 4 * lo:4 * hi]
+            )
+
+        def sums_pe(b):
+            sb = psum.tile([P, H, S4], F32, tag="tr", name="sb", bufs=3)
+            for j in range(S4):
+                fv = f_sb[b][:, j, :].rearrange("p (h r) -> p h r", r=D // H)
+                nc.tensor.matmul(out=sb[:], lhsT=ones_bf[:], rhs=fv[:, :, 0:S4], start=(j == 0), stop=(j == S4 - 1))
+            sbs[b] = sb
+
+        def sums_small(b, eng):
+            sm = small.tile([P, H, S4], F32, name="sm")
+            ssum = small.tile([P, S4], F32, name="ssum")
+            wm = small.tile([P, S4, S4], F32, name="wm")
+            wt = small.tile([P, S4, S4], F32, name="wt")
+            gf = small.tile([P, L, S4], F32, name="gf")
+            V.tensor_tensor(
+                out=sm[:], in0=sbs[b][:], in1=ident[:, 0:P:16].unsqueeze(2).to_broadcast([P, H, S4]), op=ALU.mult
+            )
+            V.tensor_reduce(out=ssum[:], in_=sm[:].rearrange("p h t -> p t h"), axis=AX.X, op=ALU.add)
+            eng.tensor_tensor(out=wm[:], in0=tt[:], in1=ssum[:].unsqueeze(1).to_broadcast([P, S4, S4]), op=ALU.mult)
+            eng.tensor_tensor(out=wt[:], in0=wm[:], in1=uu[:, :, b, :], op=ALU.subtract)
+            G.tensor_tensor(out=gf[:], in0=ht_bf[:, L:2 * L, b, :], in1=wt[:, 1:S4, :], op=ALU.mult)
+            wts[b] = wt
+            gfs[b] = gf
+
+        def turn_fields(b, u, eng):
+            if u == 0:
+                gts[b] = work.tile([P, S4, N], F32, tag="g", name="g")
+            g = gts[b]
+            wt = wts[b]
+            fw = f_sb[b][:].bitcast(F32)
+            tf = psum.tile([P, N], F32, tag="tr", name="tf", bufs=3)
+            for j in range(S4):
+                nc.tensor.transpose(tf[:, P * j:P * (j + 1)], fw[:, j, u:D // 2:2], ident[:])
+            tfb = tf[:].bitcast(BF16).rearrange("p (n e) -> p n e", e=2)
+            for e in range(2):
+                t = 2 * u + e
+                if eng == "S":
+                    nc.scalar.activation(
+                        out=g[:, t, :], in_=tfb[:, :, e], func=ACT.Identity,
+                        scale=wt[:, 0, t:t + 1], bias=bb[:, t:t + 1],
+                    )
+                else:
+                    V.tensor_scalar(
+                        out=g[:, t, :], in0=tfb[:, :, e], scalar1=wt[:, 0, t:t + 1], scalar2=bb[:, t:t + 1],
+                        op0=ALU.mult, op1=ALU.add,
+                    )
+            if u == 1:
+                gt = g[:, :, 2 * P - 1:N:P]
+                G.tensor_tensor(out=gt, in0=gt, in1=gfs[b][:].rearrange("p x t -> p t x"), op=ALU.subtract)
+
+        def mm1(i):
+            b, j = i // S4, i % S4
+            nl = psum.tile([P, S4, P], BANK_DT, tag="nl", name="nl", bufs=2)
+            for t in range(S4):
+                nc.tensor.matmul_mx(
+                    out=nl[:, t, :],
+                    lhsT=w3q[0][:, P * t:P * (t + 1)].bitcast(FP8X4), lhsT_scale=w3q[1][:, P * t:P * (t + 1)],
+                    rhs=h2q[b][0][:, P * j:P * (j + 1)].bitcast(FP8X4), rhs_scale=h2q[b][1][:, P * j:P * (j + 1)],
+                    start=True, stop=True,
+                )
+            nls[i] = nl
+
+        def fuse(i):
+            b, j = i // S4, i % S4
+            if j == 0:
+                new_grp(("e", b), "enh")
+            V.scalar_tensor_tensor(
+                out=grp[("e", b)][:, 4 * P * j:4 * P * (j + 1)].rearrange("p (c t) -> p c t", t=S4),
+                in0=nls[i][:].rearrange("p t c -> p c t"), scalar=iw[:, 1:2],
+                in1=gts[b][:, :, P * j:P * (j + 1)].rearrange("p t c -> p c t"),
+                op0=ALU.mult, op1=ALU.add,
+            )
+
+        def quant_enh(k):
+            b, hf = k // 2, k % 2
+            quant(("e", b), enq[b], 2 * P * hf, 2 * P * (hf + 1))
+
+        def mm2(i):
+            b, j = i // S4, i % S4
+            po = psum.tile([P, D], F32, tag="po", name="po", bufs=3)
+            nc.tensor.matmul_mx(
+                out=po[:],
+                lhsT=enq[b][0][:, P * j:P * (j + 1)].bitcast(FP8X4), lhsT_scale=enq[b][1][:, P * j:P * (j + 1)],
+                rhs=owq[0][:].bitcast(FP8X4), rhs_scale=owq[1][:],
+                start=True, stop=True,
+            )
+            pos[i] = po
+
+        def out_tile(i):
+            k = i // 2
+            if k not in osb:
+                osb[k] = work.tile([P, 2, D], F32, tag="o_sb", name="o_sb", bufs=4)
+            return osb[k][:, i % 2, :]
+
+        def add_bias(i):
+            dst = out_tile(i)
+            if i in OFF:
+                nc.scalar.copy(out=dst, in_=pos[i][:])
+                for c in range(2):
+                    cs = slice(256 * c, 256 * (c + 1))
+                    G.tensor_tensor(out=dst[:, cs], in0=dst[:, cs], in1=bias_sb[:, cs], op=ALU.add)
+            else:
+                V.tensor_tensor(out=dst, in0=pos[i][:], in1=bias_sb[:], op=ALU.add)
+
+        def store(i0, i1):
+            b, j0 = i0 // S4, i0 % S4
+            ov = out[b].rearrange("(p j) o -> p j o", j=S4)
+            nc.sync.dma_start(out=ov[:, j0:j0 + i1 - i0, :], in_=osb[i0 // 2][:, i0 % 2:i0 % 2 + i1 - i0, :])
+
+        new_grp("w3", "grpw")
+        turn(w3_sb, "w3", 0, "S")
+        turn(w3_sb, "w3", 1, "S")
+        quant("w3", w3q, 0, D)
+        V.tensor_scalar(out=bb[:], in0=b3_bf[:], scalar1=iw[:, 1:2], scalar2=None, op0=ALU.mult)
+        new_grp(("h", 0), "grp")
+        turn(h2_sb[0], ("h", 0), 0, "S")
+        sums_pe(0)
+        sums_small(0, V)
+        quant(("h", 0), h2q[0], 0, 2 * P)
+        turn_fields(0, 0, "S")
+        turn_fields(0, 1, "V")
+        turn(h2_sb[0], ("h", 0), 1, "S")
+        mm1(0)
+        mm1(1)
+        new_grp("ow", "grpw")
+        turn(ow_sb, "ow", 0, "S")
+        turn(ow_sb, "ow", 1, "S")
+        sums_pe(1)
+        bias_ps = psum.tile([P, D], F32, tag="tr", name="bias_ps", bufs=3)
+        nc.tensor.matmul(out=bias_ps[:], lhsT=ones_bf[:], rhs=zrow[:], start=True, stop=True)
+        nc.scalar.copy(out=bias_sb[:], in_=bias_ps[:])
+
+        def prep(r):
+            rb, rh = r // 2, r % 2
+            if rh == 0:
+                new_grp(("h", rb), "grp")
+            turn(h2_sb[rb], ("h", rb), rh, "S")
+            turn_fields(rb, rh, "S")
+
+        for k in range(NK + 2):
+            nb = (k + 3) // 2
+            do_sums = k % 2 == 1 and nb < B
+            if do_sums:
+                sums_pe(nb)
+            if k >= 2 and (2 * k - 3) in OFF:
+                add_bias(2 * k - 3)
+            if 1 <= k and k + 2 < NK:
+                prep(k + 2)
+            if 1 <= k <= NK:
+                quant_enh(k - 1)
+            if 2 <= k + 1 < NK:
+                qb, qh = (k + 1) // 2, (k + 1) % 2
+                quant(("h", qb), h2q[qb], 2 * P * qh, 2 * P * (qh + 1))
+            if 1 <= k <= NK:
+                mm2(2 * k - 2)
+            if k < NK:
+                fuse(2 * k)
+            if k == 0:
+                quant(("h", 0), h2q[0], 2 * P, N)
+                sums_small(1, G)
+                prep(2)
+            if 2 * k + 2 < NT:
+                mm1(2 * k + 2)
+            if do_sums:
+                sums_small(nb, G)
+            if k < NK:
+                fuse(2 * k + 1)
+            if k == 0:
+                quant("ow", owq, 0, D)
+            if 2 * k + 3 < NT:
+                mm1(2 * k + 3)
+            if k >= 2:
+                add_bias(2 * k - 4)
+            if 1 <= k <= NK:
+                mm2(2 * k - 1)
+            if k == NK + 1:
+                store(2 * k - 4, 2 * k - 3)
+            if k >= 2 and (2 * k - 3) not in OFF:
+                add_bias(2 * k - 3)
+            if k == NK + 1:
+                store(2 * k - 3, 2 * k - 2)
+            elif k >= 2:
+                store(2 * k - 4, 2 * k - 2)

@@ -70,7 +70,6 @@ def tile_fieldinteractionoperators_pa_kernel(
             rv = fields[:, n, :].rearrange("b (h r) -> h b r", r=D // H)
             q.dma_start(out=ht_bf[0:P:16, x, :, :], in_=rv[:, :, 0:S4])
 
-        G.dma_start(out=b3_bf[:], in_=b3.rearrange("(p t) -> p t", t=S4))
         masks.make_identity(nc, ident[:])
         nc.sync.dma_start(out=r_bf[:], in_=inter_w.partition_broadcast(P))
         nc.sync.dma_start(out=kk_bf[0:P:16, :, 0:L], in_=corr_kernels)
@@ -80,7 +79,11 @@ def tile_fieldinteractionoperators_pa_kernel(
         load_half(w3_sb, w3_v, 1)
         load_half(h2_sb[0], h2_v[0], 0)
         nc.sync.dma_start(out=f_sb[0][:], in_=f_v[0])
+        nc.sync.dma_start(out=b3_bf[:], in_=b3.rearrange("(p t) -> p t", t=S4))
+        for x in range(L, 2 * L):
+            load_row(nc.sync, x)
         load_half(h2_sb[0], h2_v[0], 1)
+        nc.sync.dma_start(out=zrow[0:1, :], in_=out_b.rearrange("(a o) -> a o", a=1))
         nc.sync.dma_start(out=ow_sb[:], in_=ow_v)
         nc.sync.dma_start(out=f_sb[1][:], in_=f_v[1])
         load_half(h2_sb[1], h2_v[1], 0)
@@ -88,9 +91,6 @@ def tile_fieldinteractionoperators_pa_kernel(
         for b in range(2, B):
             nc.sync.dma_start(out=f_sb[b][:], in_=f_v[b])
             nc.sync.dma_start(out=h2_sb[b][:], in_=h2_v[b])
-        for x in range(L, 2 * L):
-            load_row(G, x)
-        G.dma_start(out=zrow[0:1, :], in_=out_b.rearrange("(a o) -> a o", a=1))
 
         rmax = const.tile([P, 1], F32, name="rmax")
         rd = const.tile([P, 2], F32, name="rd")
@@ -218,26 +218,26 @@ def tile_fieldinteractionoperators_pa_kernel(
                 gt = g[:, :, 2 * P - 1:N:P]
                 G.tensor_tensor(out=gt, in0=gt, in1=gfs[b][:].rearrange("p x t -> p t x"), op=ALU.subtract)
 
-        def mm1(i):
-            b, j = i // S4, i % S4
-            nl = psum.tile([P, S4, P], BANK_DT, tag="nl", name="nl", bufs=2)
+        def mm1(k):
+            b, cs = k // 2, slice(2 * P * (k % 2), 2 * P * (k % 2 + 1))
+            nl = psum.tile([P, S4, 2 * P], BANK_DT, tag="nl", name="nl", bufs=2)
             for t in range(S4):
                 nc.tensor.matmul_mx(
                     out=nl[:, t, :],
                     lhsT=w3q[0][:, P * t:P * (t + 1)].bitcast(FP8X4), lhsT_scale=w3q[1][:, P * t:P * (t + 1)],
-                    rhs=h2q[b][0][:, P * j:P * (j + 1)].bitcast(FP8X4), rhs_scale=h2q[b][1][:, P * j:P * (j + 1)],
+                    rhs=h2q[b][0][:, cs].bitcast(FP8X4), rhs_scale=h2q[b][1][:, cs],
                     start=True, stop=True,
                 )
-            nls[i] = nl
+            nls[k] = nl
 
-        def fuse(i):
-            b, j = i // S4, i % S4
-            if j == 0:
+        def fuse(k):
+            b, hf = k // 2, k % 2
+            if hf == 0:
                 new_grp(("e", b), "enh")
             V.scalar_tensor_tensor(
-                out=grp[("e", b)][:, 4 * P * j:4 * P * (j + 1)].rearrange("p (c t) -> p c t", t=S4),
-                in0=nls[i][:].rearrange("p t c -> p c t"), scalar=iw[:, 1:2],
-                in1=gts[b][:, :, P * j:P * (j + 1)].rearrange("p t c -> p c t"),
+                out=grp[("e", b)][:, 8 * P * hf:8 * P * (hf + 1)].rearrange("p (c t) -> p c t", t=S4),
+                in0=nls[k][:].rearrange("p t c -> p c t"), scalar=iw[:, 1:2],
+                in1=gts[b][:, :, 2 * P * hf:2 * P * (hf + 1)].rearrange("p t c -> p c t"),
                 op0=ALU.mult, op1=ALU.add,
             )
 
@@ -291,7 +291,6 @@ def tile_fieldinteractionoperators_pa_kernel(
         turn_fields(0, 1, "V")
         turn(h2_sb[0], ("h", 0), 1, "S")
         mm1(0)
-        mm1(1)
         new_grp("ow", "grpw")
         turn(ow_sb, "ow", 0, "S")
         turn(ow_sb, "ow", 1, "S")
@@ -324,21 +323,17 @@ def tile_fieldinteractionoperators_pa_kernel(
             if 1 <= k <= NK:
                 mm2(2 * k - 2)
             if k < NK:
-                fuse(2 * k)
+                fuse(k)
             if k == 0:
                 quant(("h", 0), h2q[0], 2 * P, N)
                 sums_small(1, G)
                 prep(2)
-            if 2 * k + 2 < NT:
-                mm1(2 * k + 2)
+            if k + 1 < NK:
+                mm1(k + 1)
             if do_sums:
                 sums_small(nb, G)
-            if k < NK:
-                fuse(2 * k + 1)
             if k == 0:
                 quant("ow", owq, 0, D)
-            if 2 * k + 3 < NT:
-                mm1(2 * k + 3)
             if k >= 2:
                 add_bias(2 * k - 4)
             if 1 <= k <= NK:

@@ -106,29 +106,31 @@ def tile_fieldinteractionoperators_pa_kernel(
         uu = const.tile([P, S4, B, S4], F32, name="uu")
         bias_sb = const.tile([P, D], F32, name="bias_sb")
         V.tensor_reduce(out=rmax[:], in_=r_bf[:], axis=AX.X, op=ALU.max)
+        V.tensor_copy(out=hh[:, 0, :, :], in_=ht_bf[:, 0, :, :])
         V.tensor_scalar(out=rd[:], in0=r_bf[:], scalar1=rmax[:, 0:1], scalar2=None, op0=ALU.subtract)
         nc.scalar.activation(out=re[:], in_=rd[:], func=ACT.Exp, accum_out=rsum[:])
+        V.tensor_tensor(out=hh[:, 1, :, :], in0=hh[:, 0, :, :], in1=ht_bf[:, 1, :, :], op=ALU.add)
+        V.tensor_tensor(out=hh[:, 2, :, :], in0=hh[:, 1, :, :], in1=ht_bf[:, 2, :, :], op=ALU.add)
         V.reciprocal(out=rinv[:], in_=rsum[:])
         V.tensor_scalar(out=iw[:], in0=re[:], scalar1=rinv[:, 0:1], scalar2=None, op0=ALU.mult)
-        for lag in range(1, L + 1):
+        for lag in (3, 2, 1):
             V.tensor_scalar(
                 out=kap[:, lag - 1, :], in0=kk_bf[:, lag - 1, :], scalar1=iw[:, 0:1],
                 scalar2=1.0 / (L * (N - lag)), op0=ALU.mult, op1=ALU.mult,
             )
         V.tensor_copy(out=tt[:, 1, :], in_=kap[:, 2, :])
-        V.tensor_tensor(out=tt[:, 2, :], in0=kap[:, 1, :], in1=tt[:, 1, :], op=ALU.add)
-        V.tensor_tensor(out=tt[:, 3, :], in0=kap[:, 0, :], in1=tt[:, 2, :], op=ALU.add)
-        V.tensor_copy(out=tt[:, 0, :], in_=tt[:, 3, :])
-        V.tensor_copy(out=hh[:, 0, :, :], in_=ht_bf[:, 0, :, :])
-        V.tensor_tensor(out=hh[:, 1, :, :], in0=hh[:, 0, :, :], in1=ht_bf[:, 1, :, :], op=ALU.add)
-        V.tensor_tensor(out=hh[:, 2, :, :], in0=hh[:, 1, :, :], in1=ht_bf[:, 2, :, :], op=ALU.add)
         V.tensor_tensor(
             out=qq[:], in0=hh[:], in1=kap[:].unsqueeze(2).to_broadcast([P, L, B, S4]), op=ALU.mult
         )
+        V.tensor_tensor(out=tt[:, 2, :], in0=kap[:, 1, :], in1=kap[:, 2, :], op=ALU.add)
         V.tensor_copy(out=uu[:, 1, :, :], in_=qq[:, 2, :, :])
-        V.tensor_tensor(out=uu[:, 2, :, :], in0=qq[:, 1, :, :], in1=uu[:, 1, :, :], op=ALU.add)
+        V.tensor_tensor(out=uu[:, 2, :, :], in0=qq[:, 1, :, :], in1=qq[:, 2, :, :], op=ALU.add)
+        V.tensor_tensor(out=tt[:, 3, :], in0=kap[:, 0, :], in1=tt[:, 2, :], op=ALU.add)
+        V.tensor_tensor(out=tt[:, 0, :], in0=kap[:, 0, :], in1=tt[:, 2, :], op=ALU.add)
         V.tensor_tensor(out=uu[:, 3, :, :], in0=qq[:, 0, :, :], in1=uu[:, 2, :, :], op=ALU.add)
-        V.tensor_scalar(out=uu[:, 0, :, :], in0=uu[:, 3, :, :], scalar1=-1.0, scalar2=None, op0=ALU.add)
+        V.scalar_tensor_tensor(
+            out=uu[:, 0, :, :], in0=qq[:, 0, :, :], scalar=-1.0, in1=uu[:, 2, :, :], op0=ALU.add, op1=ALU.add
+        )
 
         def mx_tiles(nm):
             c = const.tile([P, D], U32, name=nm + "_c", align_bytes=64)
@@ -142,6 +144,7 @@ def tile_fieldinteractionoperators_pa_kernel(
         grp = {}
         gts = {}
         sbs = {}
+        sms = {}
         wts = {}
         gfs = {}
         nls = {}
@@ -176,15 +179,19 @@ def tile_fieldinteractionoperators_pa_kernel(
                 nc.tensor.matmul(out=sb[:], lhsT=ones_bf[:], rhs=fv[:, :, 0:S4], start=(j == 0), stop=(j == S4 - 1))
             sbs[b] = sb
 
-        def sums_small(b, eng):
+        def sums_mask(b):
             sm = small.tile([P, H, S4], F32, name="sm")
+            V.tensor_tensor(
+                out=sm[:], in0=sbs[b][:], in1=ident[:, 0:P:16].unsqueeze(2).to_broadcast([P, H, S4]), op=ALU.mult
+            )
+            sms[b] = sm
+
+        def sums_small(b, eng):
+            sm = sms[b]
             ssum = small.tile([P, S4], F32, name="ssum")
             wm = small.tile([P, S4, S4], F32, name="wm")
             wt = small.tile([P, S4, S4], F32, name="wt")
             gf = small.tile([P, L, S4], F32, name="gf")
-            V.tensor_tensor(
-                out=sm[:], in0=sbs[b][:], in1=ident[:, 0:P:16].unsqueeze(2).to_broadcast([P, H, S4]), op=ALU.mult
-            )
             V.tensor_reduce(out=ssum[:], in_=sm[:].rearrange("p h t -> p t h"), axis=AX.X, op=ALU.add)
             eng.tensor_tensor(out=wm[:], in0=tt[:], in1=ssum[:].unsqueeze(1).to_broadcast([P, S4, S4]), op=ALU.mult)
             eng.tensor_tensor(out=wt[:], in0=wm[:], in1=uu[:, :, b, :], op=ALU.subtract)
@@ -281,12 +288,13 @@ def tile_fieldinteractionoperators_pa_kernel(
         turn(w3_sb, "w3", 0, "S")
         turn(w3_sb, "w3", 1, "S")
         quant("w3", w3q, 0, D)
-        V.tensor_scalar(out=bb[:], in0=b3_bf[:], scalar1=iw[:, 1:2], scalar2=None, op0=ALU.mult)
         new_grp(("h", 0), "grp")
         turn(h2_sb[0], ("h", 0), 0, "S")
         sums_pe(0)
-        sums_small(0, V)
+        sums_mask(0)
         quant(("h", 0), h2q[0], 0, 2 * P)
+        V.tensor_scalar(out=bb[:], in0=b3_bf[:], scalar1=iw[:, 1:2], scalar2=None, op0=ALU.mult)
+        sums_small(0, V)
         turn_fields(0, 0, "S")
         turn_fields(0, 1, "V")
         turn(h2_sb[0], ("h", 0), 1, "S")
@@ -326,16 +334,19 @@ def tile_fieldinteractionoperators_pa_kernel(
                 fuse(k)
             if k == 0:
                 quant(("h", 0), h2q[0], 2 * P, N)
+                sums_mask(1)
                 sums_small(1, G)
                 prep(2)
             if k + 1 < NK:
                 mm1(k + 1)
             if do_sums:
-                sums_small(nb, G)
+                sums_mask(nb)
             if k == 0:
                 quant("ow", owq, 0, D)
             if k >= 2:
                 add_bias(2 * k - 4)
+            if do_sums:
+                sums_small(nb, G)
             if 1 <= k <= NK:
                 mm2(2 * k - 1)
             if k == NK + 1:

@@ -139,8 +139,9 @@ def tile_fieldinteractionoperators_pa_kernel(
 
         w3q = mx_tiles("w3")
         owq = mx_tiles("ow")
-        h2q = [mx_tiles("h2_%d" % b) for b in range(B)]
-        enq = [mx_tiles("en_%d" % b) for b in range(B)]
+        h2q0 = mx_tiles("h2_0")
+        cq = dict((k, mx_tiles("cq_%d" % k)) for k in range(1, NK + 1))
+        cmb = {}
         grp = {}
         gts = {}
         sbs = {}
@@ -154,14 +155,22 @@ def tile_fieldinteractionoperators_pa_kernel(
         def new_grp(key, tag):
             grp[key] = work.tile([P, 4 * D], BF16, tag=tag, name=tag, align_bytes=64)
 
+        def get_cmb(k):
+            if k not in cmb:
+                cmb[k] = work.tile([P, 4 * D], BF16, tag="cmb", name="cmb", bufs=3, align_bytes=64)
+            return cmb[k]
+
         def turn(src, key, half, eng):
             words = src[:].bitcast(F32)
-            gw = grp[key][:].bitcast(F32)
+            if key[0] == "c":
+                gw = get_cmb(key[1])[:].bitcast(F32)[:, 512:1024]
+            else:
+                gw = grp[key][:].bitcast(F32)[:, 512 * half:512 * (half + 1)]
             tp = psum.tile([P, 2, 2, P], F32, tag="tr", name="tp", bufs=3)
             for s2 in range(2):
                 for u in range(2):
                     nc.tensor.transpose(tp[:, s2, u, :], words[:, 2 * half + s2, u:D // 2:2], ident[:])
-            dst = gw[:, 512 * half:512 * (half + 1)].rearrange("p (s m u) -> p s m u", s=2, u=2)
+            dst = gw.rearrange("p (s m u) -> p s m u", s=2, u=2)
             if eng == "S":
                 nc.scalar.copy(out=dst, in_=tp[:].rearrange("p s u m -> p s m u"))
             else:
@@ -226,38 +235,38 @@ def tile_fieldinteractionoperators_pa_kernel(
                 G.tensor_tensor(out=gt, in0=gt, in1=gfs[b][:].rearrange("p x t -> p t x"), op=ALU.subtract)
 
         def mm1(k):
-            b, cs = k // 2, slice(2 * P * (k % 2), 2 * P * (k % 2 + 1))
+            hq, cs = (h2q0, slice(2 * P * k, 2 * P * (k + 1))) if k < 2 else (cq[k - 1], slice(2 * P, 4 * P))
             nl = psum.tile([P, S4, 2 * P], BANK_DT, tag="nl", name="nl", bufs=2)
             for t in range(S4):
                 nc.tensor.matmul_mx(
                     out=nl[:, t, :],
                     lhsT=w3q[0][:, P * t:P * (t + 1)].bitcast(FP8X4), lhsT_scale=w3q[1][:, P * t:P * (t + 1)],
-                    rhs=h2q[b][0][:, cs].bitcast(FP8X4), rhs_scale=h2q[b][1][:, cs],
+                    rhs=hq[0][:, cs].bitcast(FP8X4), rhs_scale=hq[1][:, cs],
                     start=True, stop=True,
                 )
             nls[k] = nl
 
         def fuse(k):
             b, hf = k // 2, k % 2
-            if hf == 0:
-                new_grp(("e", b), "enh")
             V.scalar_tensor_tensor(
-                out=grp[("e", b)][:, 8 * P * hf:8 * P * (hf + 1)].rearrange("p (c t) -> p c t", t=S4),
+                out=get_cmb(k + 1)[:, 0:8 * P].rearrange("p (c t) -> p c t", t=S4),
                 in0=nls[k][:].rearrange("p t c -> p c t"), scalar=iw[:, 1:2],
                 in1=gts[b][:, :, 2 * P * hf:2 * P * (hf + 1)].rearrange("p t c -> p c t"),
                 op0=ALU.mult, op1=ALU.add,
             )
 
-        def quant_enh(k):
-            b, hf = k // 2, k % 2
-            quant(("e", b), enq[b], 2 * P * hf, 2 * P * (hf + 1))
+        def quant_step(k):
+            hi = 4 * P if k + 1 < NK else 2 * P
+            V.quantize_mx(
+                out=cq[k][0][:, 0:hi].bitcast(FP8X4), scales=cq[k][1][:, 0:hi], in_=cmb[k][:, 0:4 * hi]
+            )
 
         def mm2(i):
-            b, j = i // S4, i % S4
+            eq, cs = cq[i // 2 + 1], slice(P * (i % 2), P * (i % 2 + 1))
             po = psum.tile([P, D], F32, tag="po", name="po", bufs=3)
             nc.tensor.matmul_mx(
                 out=po[:],
-                lhsT=enq[b][0][:, P * j:P * (j + 1)].bitcast(FP8X4), lhsT_scale=enq[b][1][:, P * j:P * (j + 1)],
+                lhsT=eq[0][:, cs].bitcast(FP8X4), lhsT_scale=eq[1][:, cs],
                 rhs=owq[0][:].bitcast(FP8X4), rhs_scale=owq[1][:],
                 start=True, stop=True,
             )
@@ -273,9 +282,7 @@ def tile_fieldinteractionoperators_pa_kernel(
             dst = out_tile(i)
             if i in OFF:
                 nc.scalar.copy(out=dst, in_=pos[i][:])
-                for c in range(2):
-                    cs = slice(256 * c, 256 * (c + 1))
-                    G.tensor_tensor(out=dst[:, cs], in0=dst[:, cs], in1=bias_sb[:, cs], op=ALU.add)
+                G.tensor_tensor(out=dst, in0=dst, in1=bias_sb[:], op=ALU.add)
             else:
                 V.tensor_tensor(out=dst, in0=pos[i][:], in1=bias_sb[:], op=ALU.add)
 
@@ -292,7 +299,7 @@ def tile_fieldinteractionoperators_pa_kernel(
         turn(h2_sb[0], ("h", 0), 0, "S")
         sums_pe(0)
         sums_mask(0)
-        quant(("h", 0), h2q[0], 0, 2 * P)
+        quant(("h", 0), h2q0, 0, 2 * P)
         V.tensor_scalar(out=bb[:], in0=b3_bf[:], scalar1=iw[:, 1:2], scalar2=None, op0=ALU.mult)
         sums_small(0, V)
         turn_fields(0, 0, "S")
@@ -309,9 +316,7 @@ def tile_fieldinteractionoperators_pa_kernel(
 
         def prep(r):
             rb, rh = r // 2, r % 2
-            if rh == 0:
-                new_grp(("h", rb), "grp")
-            turn(h2_sb[rb], ("h", rb), rh, "S")
+            turn(h2_sb[rb], ("c", r - 1), rh, "S")
             turn_fields(rb, rh, "S")
 
         for k in range(NK + 2):
@@ -324,16 +329,13 @@ def tile_fieldinteractionoperators_pa_kernel(
             if 1 <= k and k + 2 < NK:
                 prep(k + 2)
             if 1 <= k <= NK:
-                quant_enh(k - 1)
-            if 2 <= k + 1 < NK:
-                qb, qh = (k + 1) // 2, (k + 1) % 2
-                quant(("h", qb), h2q[qb], 2 * P * qh, 2 * P * (qh + 1))
+                quant_step(k)
             if 1 <= k <= NK:
                 mm2(2 * k - 2)
             if k < NK:
                 fuse(k)
             if k == 0:
-                quant(("h", 0), h2q[0], 2 * P, N)
+                quant(("h", 0), h2q0, 2 * P, N)
                 sums_mask(1)
                 sums_small(1, G)
                 prep(2)

@@ -55,9 +55,9 @@ def tile_fieldinteractionoperators_pa_kernel(
         dm1 = const.tile([P, 1], F32, name="dm1")
 
         V.memset(dm0[:], 0.0)
-        nc.scalar.activation(out=dm1[:], in_=dm0[:], func=ACT.Exp)
-        V.memset(kk_bf[:], 0.0)
-        V.memset(ht_bf[:], 0.0)
+        nc.scalar.activation(out=dm1[:], in_=dm0[:], func=ACT.Sigmoid)
+        G.memset(kk_bf[:], 0.0)
+        G.memset(ht_bf[:], 0.0)
         V.memset(ones_bf[:], 1.0)
         V.memset(zrow[:], 0.0)
 
@@ -92,45 +92,40 @@ def tile_fieldinteractionoperators_pa_kernel(
             nc.sync.dma_start(out=f_sb[b][:], in_=f_v[b])
             nc.sync.dma_start(out=h2_sb[b][:], in_=h2_v[b])
 
-        rmax = const.tile([P, 1], F32, name="rmax")
         rd = const.tile([P, 2], F32, name="rd")
-        re = const.tile([P, 2], F32, name="re")
-        rsum = const.tile([P, 1], F32, name="rsum")
-        rinv = const.tile([P, 1], F32, name="rinv")
         iw = const.tile([P, 2], F32, name="iw")
         bb = const.tile([P, S4], F32, name="bb")
-        kap = const.tile([P, L, S4], F32, name="kap")
-        tt = const.tile([P, S4, S4], F32, name="tt")
+        kc = const.tile([P, L, S4], F32, name="kc")
+        kt = const.tile([P, 2 * L, S4], F32, name="kt")
         hh = const.tile([P, L, B, S4], F32, name="hh")
-        qq = const.tile([P, L, B, S4], F32, name="qq")
-        uu = const.tile([P, S4, B, S4], F32, name="uu")
+        qt = const.tile([P, 2 * L, B, S4], F32, name="qt")
         bias_sb = const.tile([P, D], F32, name="bias_sb")
-        V.tensor_reduce(out=rmax[:], in_=r_bf[:], axis=AX.X, op=ALU.max)
-        V.tensor_copy(out=hh[:, 0, :, :], in_=ht_bf[:, 0, :, :])
-        V.tensor_scalar(out=rd[:], in0=r_bf[:], scalar1=rmax[:, 0:1], scalar2=None, op0=ALU.subtract)
-        nc.scalar.activation(out=re[:], in_=rd[:], func=ACT.Exp, accum_out=rsum[:])
-        V.tensor_tensor(out=hh[:, 1, :, :], in0=hh[:, 0, :, :], in1=ht_bf[:, 1, :, :], op=ALU.add)
-        V.tensor_tensor(out=hh[:, 2, :, :], in0=hh[:, 1, :, :], in1=ht_bf[:, 2, :, :], op=ALU.add)
-        V.reciprocal(out=rinv[:], in_=rsum[:])
-        V.tensor_scalar(out=iw[:], in0=re[:], scalar1=rinv[:, 0:1], scalar2=None, op0=ALU.mult)
-        for lag in (3, 2, 1):
-            V.tensor_scalar(
-                out=kap[:, lag - 1, :], in0=kk_bf[:, lag - 1, :], scalar1=iw[:, 0:1],
-                scalar2=1.0 / (L * (N - lag)), op0=ALU.mult, op1=ALU.mult,
+        for lag in (1, 2, 3):
+            nc.scalar.activation(
+                out=kc[:, lag - 1, :], in_=kk_bf[:, lag - 1, :], func=ACT.Copy, scale=1.0 / (L * (N - lag))
             )
-        V.tensor_copy(out=tt[:, 1, :], in_=kap[:, 2, :])
+        G.tensor_copy(out=hh[:, 0, :, :], in_=ht_bf[:, 0, :, :])
+        G.tensor_tensor(out=hh[:, 1, :, :], in0=hh[:, 0, :, :], in1=ht_bf[:, 1, :, :], op=ALU.add)
+        G.tensor_tensor(out=hh[:, 2, :, :], in0=hh[:, 1, :, :], in1=ht_bf[:, 2, :, :], op=ALU.add)
+        V.tensor_tensor(out=rd[:], in0=r_bf[:], in1=r_bf[:, ::-1], op=ALU.subtract)
+        nc.scalar.activation(out=iw[:], in_=rd[:], func=ACT.Sigmoid)
+        V.tensor_scalar(out=kt[:, 0:L, :], in0=kc[:], scalar1=iw[:, 0:1], scalar2=None, op0=ALU.mult)
+        V.tensor_tensor(out=kt[:, 3, :], in0=kt[:, 1, :], in1=kt[:, 2, :], op=ALU.add)
         V.tensor_tensor(
-            out=qq[:], in0=hh[:], in1=kap[:].unsqueeze(2).to_broadcast([P, L, B, S4]), op=ALU.mult
+            out=qt[:, 0:L, :, :], in0=hh[:], in1=kt[:, 0:L, :].unsqueeze(2).to_broadcast([P, L, B, S4]), op=ALU.mult
         )
-        V.tensor_tensor(out=tt[:, 2, :], in0=kap[:, 1, :], in1=kap[:, 2, :], op=ALU.add)
-        V.tensor_copy(out=uu[:, 1, :, :], in_=qq[:, 2, :, :])
-        V.tensor_tensor(out=uu[:, 2, :, :], in0=qq[:, 1, :, :], in1=qq[:, 2, :, :], op=ALU.add)
-        V.tensor_tensor(out=tt[:, 3, :], in0=kap[:, 0, :], in1=tt[:, 2, :], op=ALU.add)
-        V.tensor_tensor(out=tt[:, 0, :], in0=kap[:, 0, :], in1=tt[:, 2, :], op=ALU.add)
-        V.tensor_tensor(out=uu[:, 3, :, :], in0=qq[:, 0, :, :], in1=uu[:, 2, :, :], op=ALU.add)
+        V.tensor_tensor(
+            out=kt[:, 4:6, :], in0=kt[:, 0:1, :].to_broadcast([P, 2, S4]), in1=kt[:, 3:4, :].to_broadcast([P, 2, S4]),
+            op=ALU.add
+        )
+        V.tensor_tensor(out=qt[:, 3, :, :], in0=qt[:, 1, :, :], in1=qt[:, 2, :, :], op=ALU.add)
+        V.tensor_tensor(out=qt[:, 4, :, :], in0=qt[:, 0, :, :], in1=qt[:, 3, :, :], op=ALU.add)
         V.scalar_tensor_tensor(
-            out=uu[:, 0, :, :], in0=qq[:, 0, :, :], scalar=-1.0, in1=uu[:, 2, :, :], op0=ALU.add, op1=ALU.add
+            out=qt[:, 5, :, :], in0=qt[:, 0, :, :], scalar=-1.0, in1=qt[:, 3, :, :], op0=ALU.add, op1=ALU.add
         )
+        tt = kt[:, 2:6, :]
+        uu = qt[:, 2:6, :, :]
+        MAIN = 3
 
         def mx_tiles(nm):
             c = const.tile([P, D], U32, name=nm + "_c", align_bytes=64)
@@ -202,9 +197,9 @@ def tile_fieldinteractionoperators_pa_kernel(
             wt = small.tile([P, S4, S4], F32, name="wt")
             gf = small.tile([P, L, S4], F32, name="gf")
             V.tensor_reduce(out=ssum[:], in_=sm[:].rearrange("p h t -> p t h"), axis=AX.X, op=ALU.add)
-            eng.tensor_tensor(out=wm[:], in0=tt[:], in1=ssum[:].unsqueeze(1).to_broadcast([P, S4, S4]), op=ALU.mult)
+            eng.tensor_tensor(out=wm[:], in0=tt, in1=ssum[:].unsqueeze(1).to_broadcast([P, S4, S4]), op=ALU.mult)
             eng.tensor_tensor(out=wt[:], in0=wm[:], in1=uu[:, :, b, :], op=ALU.subtract)
-            G.tensor_tensor(out=gf[:], in0=ht_bf[:, L:2 * L, b, :], in1=wt[:, 1:S4, :], op=ALU.mult)
+            G.tensor_tensor(out=gf[:], in0=ht_bf[:, L:2 * L, b, :], in1=wt[:, 0:L, :], op=ALU.mult)
             wts[b] = wt
             gfs[b] = gf
 
@@ -223,11 +218,11 @@ def tile_fieldinteractionoperators_pa_kernel(
                 if eng == "S":
                     nc.scalar.activation(
                         out=g[:, t, :], in_=tfb[:, :, e], func=ACT.Identity,
-                        scale=wt[:, 0, t:t + 1], bias=bb[:, t:t + 1],
+                        scale=wt[:, MAIN, t:t + 1], bias=bb[:, t:t + 1],
                     )
                 else:
                     V.tensor_scalar(
-                        out=g[:, t, :], in0=tfb[:, :, e], scalar1=wt[:, 0, t:t + 1], scalar2=bb[:, t:t + 1],
+                        out=g[:, t, :], in0=tfb[:, :, e], scalar1=wt[:, MAIN, t:t + 1], scalar2=bb[:, t:t + 1],
                         op0=ALU.mult, op1=ALU.add,
                     )
             if u == 1:
@@ -300,7 +295,7 @@ def tile_fieldinteractionoperators_pa_kernel(
         sums_pe(0)
         sums_mask(0)
         quant(("h", 0), h2q0, 0, 2 * P)
-        V.tensor_scalar(out=bb[:], in0=b3_bf[:], scalar1=iw[:, 1:2], scalar2=None, op0=ALU.mult)
+        nc.scalar.activation(out=bb[:], in_=b3_bf[:], func=ACT.Copy, scale=iw[:, 1:2])
         sums_small(0, V)
         turn_fields(0, 0, "S")
         turn_fields(0, 1, "V")

from contextlib import ExitStack

import concourse.masks as masks
import concourse.mybir as mybir

F32 = mybir.dt.float32
BF16 = mybir.dt.bfloat16
U32 = mybir.dt.uint32
U8 = mybir.dt.uint8
FP8X4 = mybir.dt.float8_e4m3fn_x4
ALU = mybir.AluOpType
ACT = mybir.ActivationFunctionType
AX = mybir.AxisListType

B, N, D, H, L = 4, 512, 512, 8, 3
P = 128
S4 = 4
NT = B * S4
NK = NT // 2
FLOPS = 2 * 2 * B * N * D * D
BANK_DT = BF16
OFF = (1, 3, 5, 7, 9, 11, 13)


def tile_fieldinteractionoperators_pa_kernel(
    tc, fields, h2, corr_kernels, w3, b3, out_w, out_b, inter_w, out
):
    nc = tc.nc
    V = nc.vector
    G = nc.gpsimd
    with ExitStack() as ctx:
        const = ctx.enter_context(tc.tile_pool(name="const", bufs=1))
        loads = ctx.enter_context(tc.tile_pool(name="loads", bufs=1))
        work = ctx.enter_context(tc.tile_pool(name="work", bufs=2))
        small = ctx.enter_context(tc.tile_pool(name="small", bufs=2))
        psum = ctx.enter_context(tc.psum_pool(name="psum", bufs=2))
        ctx.enter_context(tc.manual_schedule())

        w3_sb = loads.tile([P, S4, D], BF16, name="w3_sb")
        ow_sb = loads.tile([P, S4, D], BF16, name="ow_sb")
        h2_sb = [loads.tile([P, S4, D], BF16, name="h2_sb%d" % b) for b in range(B)]
        f_sb = [loads.tile([P, S4, D], BF16, name="f_sb%d" % b) for b in range(B)]
        w3_v = w3.rearrange("(m t) k -> m t k", t=S4)
        ow_v = out_w.rearrange("(r m) c -> m r c", m=P)
        h2_v = [h2[b].rearrange("(p j) k -> p j k", j=S4) for b in range(B)]
        f_v = [fields[b].rearrange("(p j) c -> p j c", j=S4) for b in range(B)]
        r_bf = const.tile([P, 2], BF16, name="r_bf")
        b3_bf = const.tile([P, S4], BF16, name="b3_bf")
        kk_bf = const.tile([P, L, S4], BF16, name="kk_bf")
        ht_bf = const.tile([P, 2 * L, B, S4], BF16, name="ht_bf")
        zrow = const.tile([P, D], BF16, name="zrow")
        ones_bf = const.tile([P, P], BF16, name="ones_bf")
        ident = const.tile([P, P], F32, name="ident")
        dm0 = const.tile([P, 1], F32, name="dm0")
        dm1 = const.tile([P, 1], F32, name="dm1")

        V.memset(dm0[:], 0.0)
        nc.scalar.activation(out=dm1[:], in_=dm0[:], func=ACT.Sigmoid)
        G.memset(kk_bf[:], 0.0)
        G.memset(ht_bf[:], 0.0)
        V.memset(ones_bf[:], 1.0)
        V.memset(zrow[:], 0.0)

        def load_half(dst, src, half):
            sl = slice(2 * half, 2 * half + 2)
            nc.sync.dma_start(out=dst[:, sl, :], in_=src[:, sl, :])

        def load_row(q, x):
            n = x if x < L else N - 2 * L + x
            rv = fields[:, n, :].rearrange("b (h r) -> h b r", r=D // H)
            q.dma_start(out=ht_bf[0:P:16, x, :, :], in_=rv[:, :, 0:S4])

        masks.make_identity(nc, ident[:])
        nc.sync.dma_start(out=r_bf[:], in_=inter_w.partition_broadcast(P))
        nc.sync.dma_start(out=kk_bf[0:P:16, :, 0:L], in_=corr_kernels)
        for x in range(L):
            load_row(nc.sync, x)
        load_half(w3_sb, w3_v, 0)
        load_half(w3_sb, w3_v, 1)
        load_half(h2_sb[0], h2_v[0], 0)
        nc.sync.dma_start(out=f_sb[0][:], in_=f_v[0])
        nc.sync.dma_start(out=b3_bf[:], in_=b3.rearrange("(p t) -> p t", t=S4))
        for x in range(L, 2 * L):
            load_row(nc.sync, x)
        load_half(h2_sb[0], h2_v[0], 1)
        nc.sync.dma_start(out=zrow[0:1, :], in_=out_b.rearrange("(a o) -> a o", a=1))
        nc.sync.dma_start(out=ow_sb[:], in_=ow_v)
        nc.sync.dma_start(out=f_sb[1][:], in_=f_v[1])
        load_half(h2_sb[1], h2_v[1], 0)
        load_half(h2_sb[1], h2_v[1], 1)
        for b in range(2, B):
            nc.sync.dma_start(out=f_sb[b][:], in_=f_v[b])
            nc.sync.dma_start(out=h2_sb[b][:], in_=h2_v[b])

        rd = const.tile([P, 2], F32, name="rd")
        iw = const.tile([P, 2], F32, name="iw")
        bb = const.tile([P, S4], F32, name="bb")
        kc = const.tile([P, L, S4], F32, name="kc")
        kt = const.tile([P, 2 * L, S4], F32, name="kt")
        hh = const.tile([P, L, B, S4], F32, name="hh")
        qt = const.tile([P, 2 * L, B, S4], F32, name="qt")
        bias_sb = const.tile([P, D], F32, name="bias_sb")
        for lag in (1, 2, 3):
            nc.scalar.activation(
                out=kc[:, lag - 1, :], in_=kk_bf[:, lag - 1, :], func=ACT.Copy, scale=1.0 / (L * (N - lag))
            )
        G.tensor_copy(out=hh[:, 0, :, :], in_=ht_bf[:, 0, :, :])
        G.tensor_tensor(out=hh[:, 1, :, :], in0=hh[:, 0, :, :], in1=ht_bf[:, 1, :, :], op=ALU.add)
        G.tensor_tensor(out=hh[:, 2, :, :], in0=hh[:, 1, :, :], in1=ht_bf[:, 2, :, :], op=ALU.add)
        V.tensor_tensor(out=rd[:], in0=r_bf[:], in1=r_bf[:, ::-1], op=ALU.subtract)
        nc.scalar.activation(out=iw[:], in_=rd[:], func=ACT.Sigmoid)
        V.tensor_scalar(out=kt[:, 0:L, :], in0=kc[:], scalar1=iw[:, 0:1], scalar2=None, op0=ALU.mult)
        V.tensor_tensor(out=kt[:, 3, :], in0=kt[:, 1, :], in1=kt[:, 2, :], op=ALU.add)
        V.tensor_tensor(
            out=qt[:, 0:L, :, :], in0=hh[:], in1=kt[:, 0:L, :].unsqueeze(2).to_broadcast([P, L, B, S4]), op=ALU.mult
        )
        V.tensor_tensor(
            out=kt[:, 4:6, :], in0=kt[:, 0:1, :].to_broadcast([P, 2, S4]), in1=kt[:, 3:4, :].to_broadcast([P, 2, S4]),
            op=ALU.add
        )
        V.tensor_tensor(out=qt[:, 3, :, :], in0=qt[:, 1, :, :], in1=qt[:, 2, :, :], op=ALU.add)
        V.tensor_tensor(out=qt[:, 4, :, :], in0=qt[:, 0, :, :], in1=qt[:, 3, :, :], op=ALU.add)
        V.scalar_tensor_tensor(
            out=qt[:, 5, :, :], in0=qt[:, 0, :, :], scalar=-1.0, in1=qt[:, 3, :, :], op0=ALU.add, op1=ALU.add
        )
        tt = kt[:, 2:6, :]
        uu = qt[:, 2:6, :, :]
        MAIN = 3

        def mx_tiles(nm):
            c = const.tile([P, D], U32, name=nm + "_c", align_bytes=64)
            s = const.tile([P, D], U8, name=nm + "_s", align_bytes=64)
            return c, s

        w3q = mx_tiles("w3")
        owq = mx_tiles("ow")
        h2q0 = mx_tiles("h2_0")
        cq = dict((k, mx_tiles("cq_%d" % k)) for k in range(1, NK + 1))
        cmb = {}
        grp = {}
        gts = {}
        sbs = {}
        sms = {}
        wts = {}
        gfs = {}
        nls = {}
        pos = {}
        osb = {}

        def new_grp(key, tag):
            grp[key] = work.tile([P, 4 * D], BF16, tag=tag, name=tag, align_bytes=64)

        def get_cmb(k):
            if k not in cmb:
                cmb[k] = work.tile([P, 4 * D], BF16, tag="cmb", name="cmb", bufs=3, align_bytes=64)
            return cmb[k]

        def turn(src, key, half, eng):
            words = src[:].bitcast(F32)
            if key[0] == "c":
                gw = get_cmb(key[1])[:].bitcast(F32)[:, 512:1024]
            else:
                gw = grp[key][:].bitcast(F32)[:, 512 * half:512 * (half + 1)]
            tp = psum.tile([P, 2, 2, P], F32, tag="tr", name="tp", bufs=3)
            for s2 in range(2):
                for u in range(2):
                    nc.tensor.transpose(tp[:, s2, u, :], words[:, 2 * half + s2, u:D // 2:2], ident[:])
            dst = gw.rearrange("p (s m u) -> p s m u", s=2, u=2)
            if eng == "S":
                nc.scalar.copy(out=dst, in_=tp[:].rearrange("p s u m -> p s m u"))
            else:
                V.tensor_copy(out=dst, in_=tp[:].rearrange("p s u m -> p s m u"))

        def quant(key, q, lo, hi):
            V.quantize_mx(
                out=q[0][:, lo:hi].bitcast(FP8X4), scales=q[1][:, lo:hi], in_=grp[key][:, 4 * lo:4 * hi]
            )

        def sums_pe(b):
            sb = psum.tile([P, H, S4], F32, tag="tr", name="sb", bufs=3)
            for j in range(S4):
                fv = f_sb[b][:, j, :].rearrange("p (h r) -> p h r", r=D // H)
                nc.tensor.matmul(out=sb[:], lhsT=ones_bf[:], rhs=fv[:, :, 0:S4], start=(j == 0), stop=(j == S4 - 1))
            sbs[b] = sb

        def sums_mask(b):
            sm = small.tile([P, H, S4], F32, name="sm")
            V.tensor_tensor(
                out=sm[:], in0=sbs[b][:], in1=ident[:, 0:P:16].unsqueeze(2).to_broadcast([P, H, S4]), op=ALU.mult
            )
            sms[b] = sm

        def sums_small(b, eng):
            sm = sms[b]
            ssum = small.tile([P, S4], F32, name="ssum")
            wm = small.tile([P, S4, S4], F32, name="wm")
            wt = small.tile([P, S4, S4], F32, name="wt")
            gf = small.tile([P, L, S4], F32, name="gf")
            V.tensor_reduce(out=ssum[:], in_=sm[:].rearrange("p h t -> p t h"), axis=AX.X, op=ALU.add)
            eng.tensor_tensor(out=wm[:], in0=tt, in1=ssum[:].unsqueeze(1).to_broadcast([P, S4, S4]), op=ALU.mult)
            eng.tensor_tensor(out=wt[:], in0=wm[:], in1=uu[:, :, b, :], op=ALU.subtract)
            G.tensor_tensor(out=gf[:], in0=ht_bf[:, L:2 * L, b, :], in1=wt[:, 0:L, :], op=ALU.mult)
            wts[b] = wt
            gfs[b] = gf

        def turn_fields(b, u, eng):
            if u == 0:
                gts[b] = work.tile([P, S4, N], F32, tag="g", name="g")
            g = gts[b]
            wt = wts[b]
            fw = f_sb[b][:].bitcast(F32)
            tf = psum.tile([P, N], F32, tag="tr", name="tf", bufs=3)
            for j in range(S4):
                nc.tensor.transpose(tf[:, P * j:P * (j + 1)], fw[:, j, u:D // 2:2], ident[:])
            tfb = tf[:].bitcast(BF16).rearrange("p (n e) -> p n e", e=2)
            for e in range(2):
                t = 2 * u + e
                if eng == "S":
                    nc.scalar.activation(
                        out=g[:, t, :], in_=tfb[:, :, e], func=ACT.Identity,
                        scale=wt[:, MAIN, t:t + 1], bias=bb[:, t:t + 1],
                    )
                else:
                    V.tensor_scalar(
                        out=g[:, t, :], in0=tfb[:, :, e], scalar1=wt[:, MAIN, t:t + 1], scalar2=bb[:, t:t + 1],
                        op0=ALU.mult, op1=ALU.add,
                    )
            if u == 1:
                gt = g[:, :, 2 * P - 1:N:P]
                G.tensor_tensor(out=gt, in0=gt, in1=gfs[b][:].rearrange("p x t -> p t x"), op=ALU.subtract)

        def mm1(k):
            hq, cs = (h2q0, slice(2 * P * k, 2 * P * (k + 1))) if k < 2 else (cq[k - 1], slice(2 * P, 4 * P))
            nl = psum.tile([P, S4, 2 * P], BANK_DT, tag="nl", name="nl", bufs=2)
            for t in range(S4):
                nc.tensor.matmul_mx(
                    out=nl[:, t, :],
                    lhsT=w3q[0][:, P * t:P * (t + 1)].bitcast(FP8X4), lhsT_scale=w3q[1][:, P * t:P * (t + 1)],
                    rhs=hq[0][:, cs].bitcast(FP8X4), rhs_scale=hq[1][:, cs],
                    start=True, stop=True,
                )
            nls[k] = nl

        def fuse(k):
            b, hf = k // 2, k % 2
            V.scalar_tensor_tensor(
                out=get_cmb(k + 1)[:, 0:8 * P].rearrange("p (c t) -> p c t", t=S4),
                in0=nls[k][:].rearrange("p t c -> p c t"), scalar=iw[:, 1:2],
                in1=gts[b][:, :, 2 * P * hf:2 * P * (hf + 1)].rearrange("p t c -> p c t"),
                op0=ALU.mult, op1=ALU.add,
            )

        def quant_step(k):
            hi = 4 * P if k + 1 < NK else 2 * P
            V.quantize_mx(
                out=cq[k][0][:, 0:hi].bitcast(FP8X4), scales=cq[k][1][:, 0:hi], in_=cmb[k][:, 0:4 * hi]
            )

        def mm2(i):
            eq, cs = cq[i // 2 + 1], slice(P * (i % 2), P * (i % 2 + 1))
            po = psum.tile([P, D], F32, tag="po", name="po", bufs=3)
            nc.tensor.matmul_mx(
                out=po[:],
                lhsT=eq[0][:, cs].bitcast(FP8X4), lhsT_scale=eq[1][:, cs],
                rhs=owq[0][:].bitcast(FP8X4), rhs_scale=owq[1][:],
                start=True, stop=True,
            )
            pos[i] = po

        def out_tile(i):
            k = i // 2
            if k not in osb:
                osb[k] = work.tile([P, 2, D], F32, tag="o_sb", name="o_sb", bufs=4)
            return osb[k][:, i % 2, :]

        def add_bias(i):
            dst = out_tile(i)
            if i in OFF:
                nc.scalar.copy(out=dst, in_=pos[i][:])
                G.tensor_tensor(out=dst, in0=dst, in1=bias_sb[:], op=ALU.add)
            else:
                V.tensor_tensor(out=dst, in0=pos[i][:], in1=bias_sb[:], op=ALU.add)

        def store(i0, i1):
            b, j0 = i0 // S4, i0 % S4
            ov = out[b].rearrange("(p j) o -> p j o", j=S4)
            nc.sync.dma_start(out=ov[:, j0:j0 + i1 - i0, :], in_=osb[i0 // 2][:, i0 % 2:i0 % 2 + i1 - i0, :])

        new_grp("w3", "grpw")
        turn(w3_sb, "w3", 0, "S")
        turn(w3_sb, "w3", 1, "S")
        quant("w3", w3q, 0, D)
        new_grp(("h", 0), "grp")
        turn(h2_sb[0], ("h", 0), 0, "S")
        sums_pe(0)
        sums_mask(0)
        quant(("h", 0), h2q0, 0, 2 * P)
        nc.scalar.activation(out=bb[:], in_=b3_bf[:], func=ACT.Copy, scale=iw[:, 1:2])
        sums_small(0, V)
        turn_fields(0, 0, "S")
        turn_fields(0, 1, "V")
        turn(h2_sb[0], ("h", 0), 1, "S")
        mm1(0)
        new_grp("ow", "grpw")
        turn(ow_sb, "ow", 0, "S")
        turn(ow_sb, "ow", 1, "S")
        sums_pe(1)
        bias_ps = psum.tile([P, D], F32, tag="tr", name="bias_ps", bufs=3)
        nc.tensor.matmul(out=bias_ps[:], lhsT=ones_bf[:], rhs=zrow[:], start=True, stop=True)
        nc.scalar.copy(out=bias_sb[:], in_=bias_ps[:])

        def prep(r):
            rb, rh = r // 2, r % 2
            turn(h2_sb[rb], ("c", r - 1), rh, "S")
            turn_fields(rb, rh, "S")

        for k in range(NK + 2):
            nb = (k + 3) // 2
            do_sums = k % 2 == 1 and nb < B
            if do_sums:
                sums_pe(nb)
            if k >= 2 and (2 * k - 3) in OFF:
                add_bias(2 * k - 3)
            if 1 <= k and k + 2 < NK:
                prep(k + 2)
            if 1 <= k <= NK:
                quant_step(k)
            if 1 <= k <= NK:
                mm2(2 * k - 2)
            if k < NK:
                fuse(k)
            if k == 0:
                quant(("h", 0), h2q0, 2 * P, N)
                sums_mask(1)
                sums_small(1, G)
                prep(2)
            if k + 1 < NK:
                mm1(k + 1)
            if do_sums:
                sums_mask(nb)
            if k == 0:
                quant("ow", owq, 0, D)
            if k >= 2:
                add_bias(2 * k - 4)
            if do_sums:
                sums_small(nb, G)
            if 1 <= k <= NK:
                mm2(2 * k - 1)
            if k == NK + 1:
                store(2 * k - 4, 2 * k - 3)
            if k >= 2 and (2 * k - 3) not in OFF:
                add_bias(2 * k - 3)
            if k == NK + 1:
                store(2 * k - 3, 2 * k - 2)
            elif k >= 2:
                store(2 * k - 4, 2 * k - 2)
